import numpy as np
import ml_dtypes


def mxq(x, axis, fmt="e4m3"):
    dtype, down = {"e4m3": (ml_dtypes.float8_e4m3fn, 7), "e5m2": (ml_dtypes.float8_e5m2, 14)}[fmt]
    v = np.moveaxis(np.asarray(x, np.float32).astype(ml_dtypes.bfloat16).astype(np.float64), axis, -1)
    blocks = v.reshape(v.shape[:-1] + (-1, 32))
    amax = np.abs(blocks).max(-1, keepdims=True)
    byte = np.maximum(np.where(amax > 0, np.frexp(amax)[1] - 1 + 127, 0) - down, 1)
    scale = np.exp2(byte - 127.0)
    codes = (blocks / scale).astype(np.float32).astype(dtype).astype(np.float64)
    return np.moveaxis((codes * scale).reshape(v.shape), -1, axis)


WIDE = False


def mx_kscale(k):
    if not WIDE:
        return np.ones(k)
    levels = np.array([10, -10, 5, -5, 0])
    a = np.random.permutation(np.resize(levels, k // 512 * 4)).reshape(k // 512, 4)
    idx = np.arange(k)
    return np.exp2(a[idx // 512, idx % 128 // 32])


BF16 = ml_dtypes.bfloat16


def bf(x):
    return np.asarray(x, np.float32).astype(BF16)


def f64(x):
    return np.asarray(x).astype(np.float64)


B, D, O1, O2, O3 = 1024, 1536, 1024, 512, 128
EPS = 1e-5


def mish(v):
    return v * np.tanh(np.log(1.0 + np.exp(v)))


def sigmoid(v):
    return 1.0 / (1.0 + np.exp(-v))


def ln(u, g, b):
    mu = u.mean(-1, keepdims=True)
    var = np.square(u - mu).mean(-1, keepdims=True)
    return (u - mu) * (1.0 / np.sqrt(var + EPS)) * g + b


def setup_inputs():
    s = mx_kscale(O2)
    return {"h_dec1": bf(mish(np.random.standard_normal((B, O2))) * s),
            "D2": bf(np.random.standard_normal((O1, O2)) * 1.5 / np.sqrt(O2) / s),
            "g4": bf(1.0 + 0.1 * np.random.standard_normal(O1)),
            "b4": bf(0.1 * np.random.standard_normal(O1)),
            "D3": bf(np.random.standard_normal((D, O1)) * 1.5 / np.sqrt(O1)),
            "bo": bf(0.3 * np.random.standard_normal(D))}


def reference(h_dec1, D2, g4, b4, D3, bo):
    u = mxq(f64(h_dec1), 1, "e4m3") @ mxq(f64(D2), 1, "e4m3").T
    h = mish(ln(u, f64(g4), f64(b4)))
    return sigmoid((mxq(h, 1, "e4m3") @ mxq(f64(D3), 1, "e4m3").T) + f64(bo))

@@ -1,0 +1,241 @@
+import concourse.mybir as mybir
+from concourse.masks import make_identity
+
+F32 = mybir.dt.float32
+BF16 = mybir.dt.bfloat16
+U32 = mybir.dt.uint32
+U8 = mybir.dt.uint8
+FP8X4 = mybir.dt.float8_e4m3fn_x4
+AF = mybir.ActivationFunctionType
+ALU = mybir.AluOpType
+
+P = 128
+PACK = 4
+K_PASS = P * PACK
+BANK = 512
+UNIT = 512
+
+B, K1, O1, D_OUT = 1024, 512, 1024, 1536
+EPS = 1e-5
+B_TILES = B // P
+HALVES = B // BANK
+PASSES2 = O1 // K_PASS
+
+FLOPS = 2 * B * O1 * K1 + 2 * B * D_OUT * O1
+
+
+def regroup_unit(nc, psum, stage, ident, words, first_row_tile, first_word, copies):
+    grouped = stage.tile([P, PACK * UNIT], BF16, align_bytes=64, tag="grouped")
+    grouped_words = grouped[:].bitcast(F32).rearrange("p (h r u) -> p h r u", h=2, u=2)
+    for h in range(2):
+        bank = psum.tile([P, BANK], F32, tag="bank")
+        planes = bank[:].rearrange("p (u j r) -> p u j r", u=2, j=2)
+        for u in range(2):
+            for j in range(2):
+                nc.tensor.transpose(
+                    planes[:, u, j, :],
+                    words[:, first_row_tile + 2 * h + j, first_word + P * u : first_word + P * (u + 1)],
+                    ident[:],
+                )
+        copies[h](out=grouped_words[:, h], in_=bank[:].rearrange("p (u r) -> p r u", u=2))
+    return grouped
+
+
+def quantise_unit(nc, grouped, codes, scales):
+    nc.vector.quantize_mx(out=codes.bitcast(FP8X4), scales=scales, in_=grouped[:])
+
+
+def tile_autoencoder_pb_kernel(tc, h_dec1, D2, g4, b4, D3, bo, out):
+    nc = tc.nc
+    with (
+        tc.tile_pool(name="keep", bufs=1) as keep,
+        tc.tile_pool(name="stage", bufs=4) as stage,
+        tc.tile_pool(name="small", bufs=4) as small,
+        tc.tile_pool(name="outs", bufs=3) as outs,
+        tc.psum_pool(name="psum", bufs=8) as psum,
+    ):
+        x_raw = keep.tile([P, B_TILES * K1], BF16)
+        d2_raw = keep.tile([P, (O1 // P) * K1], BF16)
+        d3_raw = keep.tile([P, (D_OUT // P) * O1], BF16)
+        x_rows = x_raw[:].rearrange("p (i k) -> p i k", k=K1)
+        d2_rows = d2_raw[:].rearrange("p (i k) -> p i k", k=K1)
+        d3_rows = d3_raw[:].rearrange("p (i k) -> p i k", k=O1)
+        x_dram = h_dec1.rearrange("(i p) k -> p i k", p=P)
+        d2_dram = D2.rearrange("(i p) k -> p i k", p=P)
+        d3_dram = D3.rearrange("(i p) k -> p i k", p=P)
+        tiles_per_unit = UNIT // P
+        for c in range(B // UNIT):
+            rows = slice(tiles_per_unit * c, tiles_per_unit * (c + 1))
+            nc.sync.dma_start(out=x_rows[:, rows, :], in_=x_dram[:, rows, :])
+        for c in range(O1 // UNIT):
+            rows = slice(tiles_per_unit * c, tiles_per_unit * (c + 1))
+            nc.sync.dma_start(out=d2_rows[:, rows, :], in_=d2_dram[:, rows, :])
+
+        gb_raw = keep.tile([P, 2 * P], BF16)
+        nc.vector.memset(gb_raw[:], 0.0)
+        nc.scalar.dma_start(out=gb_raw[0:4, :], in_=g4.rearrange("(m w) -> m w", m=4))
+        nc.scalar.dma_start(out=gb_raw[4:8, :], in_=b4.rearrange("(m w) -> m w", m=4))
+
+        for c in range(D_OUT // UNIT):
+            rows = slice(tiles_per_unit * c, tiles_per_unit * (c + 1))
+            nc.sync.dma_start(out=d3_rows[:, rows, :], in_=d3_dram[:, rows, :])
+        bo_all = keep.tile([P, D_OUT], BF16)
+        nc.sync.dma_start(out=bo_all[:], in_=bo.partition_broadcast(P))
+
+        ident = keep.tile([P, P], F32)
+        make_identity(nc, ident[:])
+        minus_half = keep.tile([P, 1], F32)
+        nc.gpsimd.memset(minus_half[:], -0.5)
+        one = keep.tile([P, 1], F32)
+        nc.gpsimd.memset(one[:], 1.0)
+
+        x_words = x_raw[:].bitcast(F32).rearrange("p (i w) -> p i w", w=K1 // 2)
+        d2_words = d2_raw[:].bitcast(F32).rearrange("p (i w) -> p i w", w=K1 // 2)
+        d3_words = d3_raw[:].bitcast(F32).rearrange("p (i w) -> p i w", w=O1 // 2)
+
+        x_codes = keep.tile([P, B], U32, align_bytes=64)
+        x_scales = keep.tile([P, B], U8, align_bytes=64)
+        d2_codes = keep.tile([P, O1], U32, align_bytes=64)
+        d2_scales = keep.tile([P, O1], U8, align_bytes=64)
+        d3_codes = keep.tile([P, PASSES2, D_OUT], U32, align_bytes=64)
+        d3_scales = keep.tile([P, PASSES2, D_OUT], U8, align_bytes=64)
+        h_codes = keep.tile([P, PASSES2, B], U32, align_bytes=64)
+        h_scales = keep.tile([P, PASSES2, B], U8, align_bytes=64)
+
+        both = (nc.scalar.copy, nc.vector.tensor_copy)
+        x_grouped = [
+            regroup_unit(nc, psum, stage, ident, x_words, tiles_per_unit * c, 0, both)
+            for c in range(B // UNIT)
+        ]
+        d2_grouped = [
+            regroup_unit(nc, psum, stage, ident, d2_words, tiles_per_unit * c, 0, both)
+            for c in range(O1 // UNIT)
+        ]
+        for c in range(B // UNIT):
+            cols = slice(UNIT * c, UNIT * (c + 1))
+            quantise_unit(nc, x_grouped[c], x_codes[:, cols], x_scales[:, cols])
+        for c in range(O1 // UNIT):
+            cols = slice(UNIT * c, UNIT * (c + 1))
+            quantise_unit(nc, d2_grouped[c], d2_codes[:, cols], d2_scales[:, cols])
+
+        gb_bank = psum.tile([P, BANK], F32, tag="bank")
+        nc.tensor.transpose(gb_bank[:, 0:P], gb_raw[:].bitcast(F32), ident[:])
+        gain_bias = keep.tile([P, 16], F32)
+        nc.vector.tensor_copy(out=gain_bias[:], in_=gb_bank[:, 0:8].bitcast(BF16))
+
+        z = keep.tile([P, B_TILES, O1], F32)
+        for i in range(B_TILES):
+            b_cols = slice(P * i, P * (i + 1))
+            stats = small.tile([P, 2, 6], F32)
+            u_banks = []
+            for n in range(O1 // BANK):
+                o_cols = slice(BANK * n, BANK * (n + 1))
+                u = psum.tile([P, BANK], F32, tag="bank")
+                nc.tensor.matmul_mx(
+                    out=u[:],
+                    lhsT=x_codes[:, b_cols].bitcast(FP8X4),
+                    lhsT_scale=x_scales[:, b_cols],
+                    rhs=d2_codes[:, o_cols].bitcast(FP8X4),
+                    rhs_scale=d2_scales[:, o_cols],
+                    start=True,
+                    stop=True,
+                )
+                nc.vector.bn_stats(out=stats[:, n, :], in_=u[:])
+                u_banks.append(u)
+            mean_var = small.tile([P, 2], F32)
+            nc.vector.bn_aggr(out=mean_var[:], in_=stats[:].rearrange("p n s -> p (n s)"))
+            var_eps = small.tile([P, 1], F32)
+            nc.gpsimd.tensor_scalar(
+                out=var_eps[:], in0=mean_var[:, 1:2], scalar1=1.0, scalar2=EPS, op0=ALU.mult, op1=ALU.add
+            )
+            rstd = small.tile([P, 1], F32)
+            nc.gpsimd.tensor_tensor(out=rstd[:], in0=var_eps[:], in1=minus_half[:], op=ALU.pow)
+            shift = small.tile([P, 1], F32)
+            nc.gpsimd.tensor_scalar(
+                out=shift[:], in0=mean_var[:, 0:1], scalar1=rstd[:, 0:1], scalar2=-1.0, op0=ALU.mult, op1=ALU.mult
+            )
+            for n in range(O1 // BANK):
+                nc.scalar.activation(
+                    out=z[:, i, BANK * n : BANK * (n + 1)].rearrange("p (m e q) -> p m e q", m=2, e=2),
+                    in_=u_banks[n][:].rearrange("p (m q e) -> p m e q", m=2, e=2),
+                    func=AF.Identity,
+                    scale=rstd[:, 0:1],
+                    bias=shift[:, 0:1],
+                )
+
+        v = keep.tile([P, HALVES, PASSES2, PACK, BANK], F32)
+        w = keep.tile([P, HALVES, PASSES2, PACK, BANK], F32)
+        for half in range(HALVES):
+            for g in range(PASSES2):
+                for t in range(PACK):
+                    c = PACK * g + t
+                    zT = psum.tile([P, BANK], F32, tag="bank")
+                    for j in range(BANK // P):
+                        nc.tensor.transpose(
+                            zT[:, P * j : P * (j + 1)],
+                            z[:, (BANK // P) * half + j, P * c : P * (c + 1)],
+                            ident[:],
+                        )
+                    nc.vector.tensor_scalar(
+                        out=v[:, half, g, t, :],
+                        in0=zT[:],
+                        scalar1=gain_bias[:, c : c + 1],
+                        scalar2=gain_bias[:, 8 + c : 9 + c],
+                        op0=ALU.mult,
+                        op1=ALU.add,
+                    )
+                    nc.scalar.activation(out=w[:, half, g, t, :], in_=v[:, half, g, t, :], func=AF.Exp)
+
+        vector_only = (nc.vector.tensor_copy, nc.vector.tensor_copy)
+        waiting = None
+        for g in range(PASSES2):
+            for c in range(D_OUT // UNIT):
+                cols = slice(UNIT * c, UNIT * (c + 1))
+                grouped = regroup_unit(
+                    nc, psum, stage, ident, d3_words, tiles_per_unit * c, (K_PASS // 2) * g, vector_only
+                )
+                if waiting is not None:
+                    quantise_unit(nc, *waiting)
+                waiting = (grouped, d3_codes[:, g, cols], d3_scales[:, g, cols])
+        quantise_unit(nc, *waiting)
+
+        for half in range(HALVES):
+            for g in range(PASSES2):
+                chunk = w[:, half, g].rearrange("p t b -> p (t b)")
+                nc.scalar.activation(out=chunk, in_=chunk, func=AF.Ln, bias=one[:, 0:1])
+        for half in range(HALVES):
+            for g in range(PASSES2):
+                chunk = w[:, half, g].rearrange("p t b -> p (t b)")
+                nc.scalar.activation(out=chunk, in_=chunk, func=AF.Tanh)
+        for half in range(HALVES):
+            b_cols = slice(BANK * half, BANK * (half + 1))
+            for g in range(PASSES2):
+                h_grouped = stage.tile([P, PACK * BANK], BF16, align_bytes=64, tag="grouped")
+                nc.vector.tensor_tensor(
+                    out=h_grouped[:].rearrange("p (b t) -> p b t", t=PACK),
+                    in0=v[:, half, g].rearrange("p t b -> p b t"),
+                    in1=w[:, half, g].rearrange("p t b -> p b t"),
+                    op=ALU.mult,
+                )
+                quantise_unit(nc, h_grouped, h_codes[:, g, b_cols], h_scales[:, g, b_cols])
+
+        out_tiles = out.rearrange("(i p) d -> i p d", p=P)
+        for i in range(B_TILES):
+            b_cols = slice(P * i, P * (i + 1))
+            result = outs.tile([P, D_OUT], F32)
+            for n in range(D_OUT // BANK):
+                d_cols = slice(BANK * n, BANK * (n + 1))
+                acc = psum.tile([P, BANK], F32, tag="bank")
+                for g in range(PASSES2):
+                    nc.tensor.matmul_mx(
+                        out=acc[:],
+                        lhsT=h_codes[:, g, b_cols].bitcast(FP8X4),
+                        lhsT_scale=h_scales[:, g, b_cols],
+                        rhs=d3_codes[:, g, d_cols].bitcast(FP8X4),
+                        rhs_scale=d3_scales[:, g, d_cols],
+                        start=(g == 0),
+                        stop=(g == PASSES2 - 1),
+                    )
+                nc.vector.tensor_tensor(out=result[:, d_cols], in0=acc[:], in1=bo_all[:, d_cols], op=ALU.add)
+            nc.scalar.activation(out=result[:], in_=result[:], func=AF.Sigmoid)
+            nc.sync.dma_start(out=out_tiles[i], in_=result[:])

@@ -45,6 +45,28 @@ def quantise_unit(nc, grouped, codes, scales):
     nc.vector.quantize_mx(out=codes.bitcast(FP8X4), scales=scales, in_=grouped[:])
 
 
+def quantise_operand(nc, psum, stage, ident, words, codes, scales, copies):
+    passes, rows = codes.shape[1], codes.shape[2]
+    waiting = None
+    for g in range(passes):
+        for c in range(rows // UNIT):
+            cols = slice(UNIT * c, UNIT * (c + 1))
+            grouped = regroup_unit(nc, psum, stage, ident, words, (UNIT // P) * c, (K_PASS // 2) * g, copies)
+            if waiting is not None:
+                quantise_unit(nc, *waiting)
+            waiting = (grouped, codes[:, g, cols], scales[:, g, cols])
+    quantise_unit(nc, *waiting)
+
+
+def load_rows(nc, raw, dram):
+    k = dram.shape[1]
+    sbuf_rows = raw[:].rearrange("p (i k) -> p i k", k=k)
+    dram_rows = dram.rearrange("(i p) k -> p i k", p=P)
+    for c in range(dram.shape[0] // UNIT):
+        tiles = slice((UNIT // P) * c, (UNIT // P) * (c + 1))
+        nc.sync.dma_start(out=sbuf_rows[:, tiles, :], in_=dram_rows[:, tiles, :])
+
+
 def tile_autoencoder_pb_kernel(tc, h_dec1, D2, g4, b4, D3, bo, out):
     nc = tc.nc
     with (
@@ -53,34 +75,21 @@ def tile_autoencoder_pb_kernel(tc, h_dec1, D2, g4, b4, D3, bo, out):
         tc.tile_pool(name="small", bufs=4) as small,
         tc.tile_pool(name="outs", bufs=3) as outs,
         tc.psum_pool(name="psum", bufs=8) as psum,
+        tc.manual_schedule(),
     ):
         x_raw = keep.tile([P, B_TILES * K1], BF16)
         d2_raw = keep.tile([P, (O1 // P) * K1], BF16)
         d3_raw = keep.tile([P, (D_OUT // P) * O1], BF16)
-        x_rows = x_raw[:].rearrange("p (i k) -> p i k", k=K1)
-        d2_rows = d2_raw[:].rearrange("p (i k) -> p i k", k=K1)
-        d3_rows = d3_raw[:].rearrange("p (i k) -> p i k", k=O1)
-        x_dram = h_dec1.rearrange("(i p) k -> p i k", p=P)
-        d2_dram = D2.rearrange("(i p) k -> p i k", p=P)
-        d3_dram = D3.rearrange("(i p) k -> p i k", p=P)
-        tiles_per_unit = UNIT // P
-        for c in range(B // UNIT):
-            rows = slice(tiles_per_unit * c, tiles_per_unit * (c + 1))
-            nc.sync.dma_start(out=x_rows[:, rows, :], in_=x_dram[:, rows, :])
-        for c in range(O1 // UNIT):
-            rows = slice(tiles_per_unit * c, tiles_per_unit * (c + 1))
-            nc.sync.dma_start(out=d2_rows[:, rows, :], in_=d2_dram[:, rows, :])
+        load_rows(nc, d2_raw, D2)
+        load_rows(nc, x_raw, h_dec1)
+        load_rows(nc, d3_raw, D3)
+        bo_all = keep.tile([P, D_OUT], BF16)
+        nc.sync.dma_start(out=bo_all[:], in_=bo.partition_broadcast(P))
 
         gb_raw = keep.tile([P, 2 * P], BF16)
         nc.vector.memset(gb_raw[:], 0.0)
         nc.scalar.dma_start(out=gb_raw[0:4, :], in_=g4.rearrange("(m w) -> m w", m=4))
         nc.scalar.dma_start(out=gb_raw[4:8, :], in_=b4.rearrange("(m w) -> m w", m=4))
-
-        for c in range(D_OUT // UNIT):
-            rows = slice(tiles_per_unit * c, tiles_per_unit * (c + 1))
-            nc.sync.dma_start(out=d3_rows[:, rows, :], in_=d3_dram[:, rows, :])
-        bo_all = keep.tile([P, D_OUT], BF16)
-        nc.sync.dma_start(out=bo_all[:], in_=bo.partition_broadcast(P))
 
         ident = keep.tile([P, P], F32)
         make_identity(nc, ident[:])
@@ -93,30 +102,18 @@ def tile_autoencoder_pb_kernel(tc, h_dec1, D2, g4, b4, D3, bo, out):
         d2_words = d2_raw[:].bitcast(F32).rearrange("p (i w) -> p i w", w=K1 // 2)
         d3_words = d3_raw[:].bitcast(F32).rearrange("p (i w) -> p i w", w=O1 // 2)
 
-        x_codes = keep.tile([P, B], U32, align_bytes=64)
-        x_scales = keep.tile([P, B], U8, align_bytes=64)
-        d2_codes = keep.tile([P, O1], U32, align_bytes=64)
-        d2_scales = keep.tile([P, O1], U8, align_bytes=64)
+        x_codes = keep.tile([P, 1, B], U32, align_bytes=64)
+        x_scales = keep.tile([P, 1, B], U8, align_bytes=64)
+        d2_codes = keep.tile([P, 1, O1], U32, align_bytes=64)
+        d2_scales = keep.tile([P, 1, O1], U8, align_bytes=64)
         d3_codes = keep.tile([P, PASSES2, D_OUT], U32, align_bytes=64)
         d3_scales = keep.tile([P, PASSES2, D_OUT], U8, align_bytes=64)
         h_codes = keep.tile([P, PASSES2, B], U32, align_bytes=64)
         h_scales = keep.tile([P, PASSES2, B], U8, align_bytes=64)
 
         both = (nc.scalar.copy, nc.vector.tensor_copy)
-        x_grouped = [
-            regroup_unit(nc, psum, stage, ident, x_words, tiles_per_unit * c, 0, both)
-            for c in range(B // UNIT)
-        ]
-        d2_grouped = [
-            regroup_unit(nc, psum, stage, ident, d2_words, tiles_per_unit * c, 0, both)
-            for c in range(O1 // UNIT)
-        ]
-        for c in range(B // UNIT):
-            cols = slice(UNIT * c, UNIT * (c + 1))
-            quantise_unit(nc, x_grouped[c], x_codes[:, cols], x_scales[:, cols])
-        for c in range(O1 // UNIT):
-            cols = slice(UNIT * c, UNIT * (c + 1))
-            quantise_unit(nc, d2_grouped[c], d2_codes[:, cols], d2_scales[:, cols])
+        quantise_operand(nc, psum, stage, ident, d2_words, d2_codes, d2_scales, both)
+        quantise_operand(nc, psum, stage, ident, x_words, x_codes, x_scales, both)
 
         gb_bank = psum.tile([P, BANK], F32, tag="bank")
         nc.tensor.transpose(gb_bank[:, 0:P], gb_raw[:].bitcast(F32), ident[:])
@@ -133,10 +130,10 @@ def tile_autoencoder_pb_kernel(tc, h_dec1, D2, g4, b4, D3, bo, out):
                 u = psum.tile([P, BANK], F32, tag="bank")
                 nc.tensor.matmul_mx(
                     out=u[:],
-                    lhsT=x_codes[:, b_cols].bitcast(FP8X4),
-                    lhsT_scale=x_scales[:, b_cols],
-                    rhs=d2_codes[:, o_cols].bitcast(FP8X4),
-                    rhs_scale=d2_scales[:, o_cols],
+                    lhsT=x_codes[:, 0, b_cols].bitcast(FP8X4),
+                    lhsT_scale=x_scales[:, 0, b_cols],
+                    rhs=d2_codes[:, 0, o_cols].bitcast(FP8X4),
+                    rhs_scale=d2_scales[:, 0, o_cols],
                     start=True,
                     stop=True,
                 )
@@ -187,17 +184,7 @@ def tile_autoencoder_pb_kernel(tc, h_dec1, D2, g4, b4, D3, bo, out):
                     nc.scalar.activation(out=w[:, half, g, t, :], in_=v[:, half, g, t, :], func=AF.Exp)
 
         vector_only = (nc.vector.tensor_copy, nc.vector.tensor_copy)
-        waiting = None
-        for g in range(PASSES2):
-            for c in range(D_OUT // UNIT):
-                cols = slice(UNIT * c, UNIT * (c + 1))
-                grouped = regroup_unit(
-                    nc, psum, stage, ident, d3_words, tiles_per_unit * c, (K_PASS // 2) * g, vector_only
-                )
-                if waiting is not None:
-                    quantise_unit(nc, *waiting)
-                waiting = (grouped, d3_codes[:, g, cols], d3_scales[:, g, cols])
-        quantise_unit(nc, *waiting)
+        quantise_operand(nc, psum, stage, ident, d3_words, d3_codes, d3_scales, vector_only)
 
         for half in range(HALVES):
             for g in range(PASSES2):
@@ -207,35 +194,39 @@ def tile_autoencoder_pb_kernel(tc, h_dec1, D2, g4, b4, D3, bo, out):
             for g in range(PASSES2):
                 chunk = w[:, half, g].rearrange("p t b -> p (t b)")
                 nc.scalar.activation(out=chunk, in_=chunk, func=AF.Tanh)
+
+        out_tiles = out.rearrange("(i p) d -> i p d", p=P)
         for half in range(HALVES):
-            b_cols = slice(BANK * half, BANK * (half + 1))
+            h_grouped = []
             for g in range(PASSES2):
-                h_grouped = stage.tile([P, PACK * BANK], BF16, align_bytes=64, tag="grouped")
+                product = stage.tile([P, PACK * BANK], BF16, align_bytes=64, tag="grouped")
                 nc.vector.tensor_tensor(
-                    out=h_grouped[:].rearrange("p (b t) -> p b t", t=PACK),
+                    out=product[:].rearrange("p (b t) -> p b t", t=PACK),
                     in0=v[:, half, g].rearrange("p t b -> p b t"),
                     in1=w[:, half, g].rearrange("p t b -> p b t"),
                     op=ALU.mult,
                 )
-                quantise_unit(nc, h_grouped, h_codes[:, g, b_cols], h_scales[:, g, b_cols])
+                h_grouped.append(product)
+            b_half = slice(BANK * half, BANK * (half + 1))
+            for g in range(PASSES2):
+                quantise_unit(nc, h_grouped[g], h_codes[:, g, b_half], h_scales[:, g, b_half])
 
-        out_tiles = out.rearrange("(i p) d -> i p d", p=P)
-        for i in range(B_TILES):
-            b_cols = slice(P * i, P * (i + 1))
-            result = outs.tile([P, D_OUT], F32)
-            for n in range(D_OUT // BANK):
-                d_cols = slice(BANK * n, BANK * (n + 1))
-                acc = psum.tile([P, BANK], F32, tag="bank")
-                for g in range(PASSES2):
-                    nc.tensor.matmul_mx(
-                        out=acc[:],
-                        lhsT=h_codes[:, g, b_cols].bitcast(FP8X4),
-                        lhsT_scale=h_scales[:, g, b_cols],
-                        rhs=d3_codes[:, g, d_cols].bitcast(FP8X4),
-                        rhs_scale=d3_scales[:, g, d_cols],
-                        start=(g == 0),
-                        stop=(g == PASSES2 - 1),
-                    )
-                nc.vector.tensor_tensor(out=result[:, d_cols], in0=acc[:], in1=bo_all[:, d_cols], op=ALU.add)
-            nc.scalar.activation(out=result[:], in_=result[:], func=AF.Sigmoid)
-            nc.sync.dma_start(out=out_tiles[i], in_=result[:])
+            for i in range((BANK // P) * half, (BANK // P) * (half + 1)):
+                b_cols = slice(P * i, P * (i + 1))
+                result = outs.tile([P, D_OUT], F32)
+                for n in range(D_OUT // BANK):
+                    d_cols = slice(BANK * n, BANK * (n + 1))
+                    acc = psum.tile([P, BANK], F32, tag="bank")
+                    for g in range(PASSES2):
+                        nc.tensor.matmul_mx(
+                            out=acc[:],
+                            lhsT=h_codes[:, g, b_cols].bitcast(FP8X4),
+                            lhsT_scale=h_scales[:, g, b_cols],
+                            rhs=d3_codes[:, g, d_cols].bitcast(FP8X4),
+                            rhs_scale=d3_scales[:, g, d_cols],
+                            start=(g == 0),
+                            stop=(g == PASSES2 - 1),
+                        )
+                    nc.vector.tensor_tensor(out=result[:, d_cols], in0=acc[:], in1=bo_all[:, d_cols], op=ALU.add)
+                nc.scalar.activation(out=result[:], in_=result[:], func=AF.Sigmoid)
+                nc.sync.dma_start(out=out_tiles[i], in_=result[:])

@@ -73,7 +73,7 @@ def tile_autoencoder_pb_kernel(tc, h_dec1, D2, g4, b4, D3, bo, out):
         tc.tile_pool(name="keep", bufs=1) as keep,
         tc.tile_pool(name="stage", bufs=4) as stage,
         tc.tile_pool(name="small", bufs=4) as small,
-        tc.tile_pool(name="outs", bufs=3) as outs,
+        tc.tile_pool(name="rows", bufs=B_TILES) as rows,
         tc.psum_pool(name="psum", bufs=8) as psum,
         tc.manual_schedule(),
     ):
@@ -120,7 +120,7 @@ def tile_autoencoder_pb_kernel(tc, h_dec1, D2, g4, b4, D3, bo, out):
         gain_bias = keep.tile([P, 16], F32)
         nc.vector.tensor_copy(out=gain_bias[:], in_=gb_bank[:, 0:8].bitcast(BF16))
 
-        z = keep.tile([P, B_TILES, O1], F32)
+        z = []
         for i in range(B_TILES):
             b_cols = slice(P * i, P * (i + 1))
             stats = small.tile([P, 2, 6], F32)
@@ -151,9 +151,11 @@ def tile_autoencoder_pb_kernel(tc, h_dec1, D2, g4, b4, D3, bo, out):
             nc.gpsimd.tensor_scalar(
                 out=shift[:], in0=mean_var[:, 0:1], scalar1=rstd[:, 0:1], scalar2=-1.0, op0=ALU.mult, op1=ALU.mult
             )
+            z_tile = rows.tile([P, O1], F32, tag="rows")
+            z.append(z_tile)
             for n in range(O1 // BANK):
                 nc.scalar.activation(
-                    out=z[:, i, BANK * n : BANK * (n + 1)].rearrange("p (m e q) -> p m e q", m=2, e=2),
+                    out=z_tile[:, BANK * n : BANK * (n + 1)].rearrange("p (m e q) -> p m e q", m=2, e=2),
                     in_=u_banks[n][:].rearrange("p (m q e) -> p m e q", m=2, e=2),
                     func=AF.Identity,
                     scale=rstd[:, 0:1],
@@ -170,7 +172,7 @@ def tile_autoencoder_pb_kernel(tc, h_dec1, D2, g4, b4, D3, bo, out):
                     for j in range(BANK // P):
                         nc.tensor.transpose(
                             zT[:, P * j : P * (j + 1)],
-                            z[:, (BANK // P) * half + j, P * c : P * (c + 1)],
+                            z[(BANK // P) * half + j][:, P * c : P * (c + 1)],
                             ident[:],
                         )
                     nc.vector.tensor_scalar(
@@ -182,18 +184,15 @@ def tile_autoencoder_pb_kernel(tc, h_dec1, D2, g4, b4, D3, bo, out):
                         op1=ALU.add,
                     )
                     nc.scalar.activation(out=w[:, half, g, t, :], in_=v[:, half, g, t, :], func=AF.Exp)
-
-        vector_only = (nc.vector.tensor_copy, nc.vector.tensor_copy)
-        quantise_operand(nc, psum, stage, ident, d3_words, d3_codes, d3_scales, vector_only)
-
-        for half in range(HALVES):
             for g in range(PASSES2):
                 chunk = w[:, half, g].rearrange("p t b -> p (t b)")
                 nc.scalar.activation(out=chunk, in_=chunk, func=AF.Ln, bias=one[:, 0:1])
-        for half in range(HALVES):
             for g in range(PASSES2):
                 chunk = w[:, half, g].rearrange("p t b -> p (t b)")
                 nc.scalar.activation(out=chunk, in_=chunk, func=AF.Tanh)
+
+        vector_only = (nc.vector.tensor_copy, nc.vector.tensor_copy)
+        quantise_operand(nc, psum, stage, ident, d3_words, d3_codes, d3_scales, vector_only)
 
         out_tiles = out.rearrange("(i p) d -> i p d", p=P)
         for half in range(HALVES):
@@ -213,7 +212,7 @@ def tile_autoencoder_pb_kernel(tc, h_dec1, D2, g4, b4, D3, bo, out):
 
             for i in range((BANK // P) * half, (BANK // P) * (half + 1)):
                 b_cols = slice(P * i, P * (i + 1))
-                result = outs.tile([P, D_OUT], F32)
+                result = rows.tile([P, D_OUT], F32, tag="rows")
                 for n in range(D_OUT // BANK):
                     d_cols = slice(BANK * n, BANK * (n + 1))
                     acc = psum.tile([P, BANK], F32, tag="bank")
@@ -228,5 +227,5 @@ def tile_autoencoder_pb_kernel(tc, h_dec1, D2, g4, b4, D3, bo, out):
                             stop=(g == PASSES2 - 1),
                         )
                     nc.vector.tensor_tensor(out=result[:, d_cols], in0=acc[:], in1=bo_all[:, d_cols], op=ALU.add)
-                nc.scalar.activation(out=result[:], in_=result[:], func=AF.Sigmoid)
+                    nc.scalar.activation(out=result[:, d_cols], in_=result[:, d_cols], func=AF.Sigmoid)
                 nc.sync.dma_start(out=out_tiles[i], in_=result[:])

@@ -14,57 +14,55 @@ PACK = 4
 K_PASS = P * PACK
 BANK = 512
 UNIT = 512
+UNIT_TILES = UNIT // P
 
 B, K1, O1, D_OUT = 1024, 512, 1024, 1536
 EPS = 1e-5
 B_TILES = B // P
-HALVES = B // BANK
+HALF_TILES = BANK // P
 PASSES2 = O1 // K_PASS
 
 FLOPS = 2 * B * O1 * K1 + 2 * B * D_OUT * O1
 
 
-def regroup_unit(nc, psum, stage, ident, words, first_row_tile, first_word, copies):
-    grouped = stage.tile([P, PACK * UNIT], BF16, align_bytes=64, tag="grouped")
+def load_rows(nc, raw, dram_rows):
+    sbuf_rows = raw[:].rearrange("p (i k) -> p i k", k=dram_rows.shape[2])
+    for c in range(dram_rows.shape[1] // UNIT_TILES):
+        tiles = slice(UNIT_TILES * c, UNIT_TILES * (c + 1))
+        nc.sync.dma_start(out=sbuf_rows[:, tiles, :], in_=dram_rows[:, tiles, :])
+
+
+def regroup_unit(nc, psum, stage, ident, words, g, c, copies):
+    grouped = stage.tile([P, PACK * UNIT], BF16, align_bytes=64)
     grouped_words = grouped[:].bitcast(F32).rearrange("p (h r u) -> p h r u", h=2, u=2)
     for h in range(2):
         bank = psum.tile([P, BANK], F32, tag="bank")
         planes = bank[:].rearrange("p (u j r) -> p u j r", u=2, j=2)
         for u in range(2):
+            first_word = (K_PASS // 2) * g + P * u
             for j in range(2):
                 nc.tensor.transpose(
                     planes[:, u, j, :],
-                    words[:, first_row_tile + 2 * h + j, first_word + P * u : first_word + P * (u + 1)],
+                    words[:, UNIT_TILES * c + 2 * h + j, first_word : first_word + P],
                     ident[:],
                 )
         copies[h](out=grouped_words[:, h], in_=bank[:].rearrange("p (u r) -> p r u", u=2))
     return grouped
 
 
-def quantise_unit(nc, grouped, codes, scales):
-    nc.vector.quantize_mx(out=codes.bitcast(FP8X4), scales=scales, in_=grouped[:])
+def quantise_unit(nc, grouped, codes, scales, g, c):
+    cols = slice(UNIT * c, UNIT * (c + 1))
+    nc.vector.quantize_mx(out=codes[:, g, cols].bitcast(FP8X4), scales=scales[:, g, cols], in_=grouped[:])
 
 
-def quantise_operand(nc, psum, stage, ident, words, codes, scales, copies):
-    passes, rows = codes.shape[1], codes.shape[2]
+def quantise_units(nc, psum, stage, ident, words, codes, scales, units, copies):
     waiting = None
-    for g in range(passes):
-        for c in range(rows // UNIT):
-            cols = slice(UNIT * c, UNIT * (c + 1))
-            grouped = regroup_unit(nc, psum, stage, ident, words, (UNIT // P) * c, (K_PASS // 2) * g, copies)
-            if waiting is not None:
-                quantise_unit(nc, *waiting)
-            waiting = (grouped, codes[:, g, cols], scales[:, g, cols])
+    for g, c in units:
+        grouped = regroup_unit(nc, psum, stage, ident, words, g, c, copies)
+        if waiting is not None:
+            quantise_unit(nc, *waiting)
+        waiting = (grouped, codes, scales, g, c)
     quantise_unit(nc, *waiting)
-
-
-def load_rows(nc, raw, dram):
-    k = dram.shape[1]
-    sbuf_rows = raw[:].rearrange("p (i k) -> p i k", k=k)
-    dram_rows = dram.rearrange("(i p) k -> p i k", p=P)
-    for c in range(dram.shape[0] // UNIT):
-        tiles = slice((UNIT // P) * c, (UNIT // P) * (c + 1))
-        nc.sync.dma_start(out=sbuf_rows[:, tiles, :], in_=dram_rows[:, tiles, :])
 
 
 def tile_autoencoder_pb_kernel(tc, h_dec1, D2, g4, b4, D3, bo, out):
@@ -72,6 +70,7 @@ def tile_autoencoder_pb_kernel(tc, h_dec1, D2, g4, b4, D3, bo, out):
     with (
         tc.tile_pool(name="keep", bufs=1) as keep,
         tc.tile_pool(name="stage", bufs=4) as stage,
+        tc.tile_pool(name="products", bufs=4) as products,
         tc.tile_pool(name="small", bufs=4) as small,
         tc.tile_pool(name="rows", bufs=B_TILES) as rows,
         tc.psum_pool(name="psum", bufs=8) as psum,
@@ -80,9 +79,10 @@ def tile_autoencoder_pb_kernel(tc, h_dec1, D2, g4, b4, D3, bo, out):
         x_raw = keep.tile([P, B_TILES * K1], BF16)
         d2_raw = keep.tile([P, (O1 // P) * K1], BF16)
         d3_raw = keep.tile([P, (D_OUT // P) * O1], BF16)
-        load_rows(nc, d2_raw, D2)
-        load_rows(nc, x_raw, h_dec1)
-        load_rows(nc, d3_raw, D3)
+        load_rows(nc, d2_raw, D2.rearrange("(i p) k -> p i k", p=P))
+        load_rows(nc, x_raw, h_dec1.rearrange("(p i) k -> p i k", p=P))
+        load_rows(nc, d3_raw, D3.rearrange("(i p) k -> p i k", p=P))
+        out_tiles = out.rearrange("(p i) d -> i p d", p=P)
         bo_all = keep.tile([P, D_OUT], BF16)
         nc.sync.dma_start(out=bo_all[:], in_=bo.partition_broadcast(P))
 
@@ -111,17 +111,16 @@ def tile_autoencoder_pb_kernel(tc, h_dec1, D2, g4, b4, D3, bo, out):
         h_codes = keep.tile([P, PASSES2, B], U32, align_bytes=64)
         h_scales = keep.tile([P, PASSES2, B], U8, align_bytes=64)
 
-        both = (nc.scalar.copy, nc.vector.tensor_copy)
-        quantise_operand(nc, psum, stage, ident, d2_words, d2_codes, d2_scales, both)
-        quantise_operand(nc, psum, stage, ident, x_words, x_codes, x_scales, both)
-
-        gb_bank = psum.tile([P, BANK], F32, tag="bank")
-        nc.tensor.transpose(gb_bank[:, 0:P], gb_raw[:].bitcast(F32), ident[:])
         gain_bias = keep.tile([P, 16], F32)
-        nc.vector.tensor_copy(out=gain_bias[:], in_=gb_bank[:, 0:8].bitcast(BF16))
-
         z = []
-        for i in range(B_TILES):
+        v = keep.tile([P, 2, PASSES2, PACK, BANK], F32)
+        w = keep.tile([P, 2, PASSES2, PACK, BANK], F32)
+        h_grouped = {}
+
+        both = (nc.scalar.copy, nc.vector.tensor_copy)
+        vector_only = (nc.vector.tensor_copy, nc.vector.tensor_copy)
+
+        def statistics(i):
             b_cols = slice(P * i, P * (i + 1))
             stats = small.tile([P, 2, 6], F32)
             u_banks = []
@@ -151,29 +150,26 @@ def tile_autoencoder_pb_kernel(tc, h_dec1, D2, g4, b4, D3, bo, out):
             nc.gpsimd.tensor_scalar(
                 out=shift[:], in0=mean_var[:, 0:1], scalar1=rstd[:, 0:1], scalar2=-1.0, op0=ALU.mult, op1=ALU.mult
             )
+            return u_banks, rstd, shift
+
+        def normalise(u_banks, rstd, shift):
             z_tile = rows.tile([P, O1], F32, tag="rows")
             z.append(z_tile)
             for n in range(O1 // BANK):
+                z_blocks = z_tile[:, BANK * n : BANK * (n + 1)].rearrange("p (m e q) -> p m e q", m=2, e=2)
+                u_blocks = u_banks[n][:].rearrange("p (m q e) -> p m e q", m=2, e=2)
                 nc.scalar.activation(
-                    out=z_tile[:, BANK * n : BANK * (n + 1)].rearrange("p (m e q) -> p m e q", m=2, e=2),
-                    in_=u_banks[n][:].rearrange("p (m q e) -> p m e q", m=2, e=2),
-                    func=AF.Identity,
-                    scale=rstd[:, 0:1],
-                    bias=shift[:, 0:1],
+                    out=z_blocks, in_=u_blocks, func=AF.Identity, scale=rstd[:, 0:1], bias=shift[:, 0:1]
                 )
 
-        v = keep.tile([P, HALVES, PASSES2, PACK, BANK], F32)
-        w = keep.tile([P, HALVES, PASSES2, PACK, BANK], F32)
-        for half in range(HALVES):
+        def mish_factors(half):
             for g in range(PASSES2):
                 for t in range(PACK):
                     c = PACK * g + t
                     zT = psum.tile([P, BANK], F32, tag="bank")
-                    for j in range(BANK // P):
+                    for j in range(HALF_TILES):
                         nc.tensor.transpose(
-                            zT[:, P * j : P * (j + 1)],
-                            z[(BANK // P) * half + j][:, P * c : P * (c + 1)],
-                            ident[:],
+                            zT[:, P * j : P * (j + 1)], z[HALF_TILES * half + j][:, P * c : P * (c + 1)], ident[:]
                         )
                     nc.vector.tensor_scalar(
                         out=v[:, half, g, t, :],
@@ -191,26 +187,22 @@ def tile_autoencoder_pb_kernel(tc, h_dec1, D2, g4, b4, D3, bo, out):
                 chunk = w[:, half, g].rearrange("p t b -> p (t b)")
                 nc.scalar.activation(out=chunk, in_=chunk, func=AF.Tanh)
 
-        vector_only = (nc.vector.tensor_copy, nc.vector.tensor_copy)
-        quantise_operand(nc, psum, stage, ident, d3_words, d3_codes, d3_scales, vector_only)
-
-        out_tiles = out.rearrange("(i p) d -> i p d", p=P)
-        for half in range(HALVES):
-            h_grouped = []
+        def mish_products(half):
+            engines = (nc.gpsimd, nc.vector)
             for g in range(PASSES2):
-                product = stage.tile([P, PACK * BANK], BF16, align_bytes=64, tag="grouped")
-                nc.vector.tensor_tensor(
+                product = products.tile([P, PACK * BANK], BF16, align_bytes=64)
+                engines[g].tensor_tensor(
                     out=product[:].rearrange("p (b t) -> p b t", t=PACK),
                     in0=v[:, half, g].rearrange("p t b -> p b t"),
                     in1=w[:, half, g].rearrange("p t b -> p b t"),
                     op=ALU.mult,
                 )
-                h_grouped.append(product)
-            b_half = slice(BANK * half, BANK * (half + 1))
-            for g in range(PASSES2):
-                quantise_unit(nc, h_grouped[g], h_codes[:, g, b_half], h_scales[:, g, b_half])
+                h_grouped[(half, g)] = product
 
-            for i in range((BANK // P) * half, (BANK // P) * (half + 1)):
+        def second_layer(half):
+            for g in range(PASSES2):
+                quantise_unit(nc, h_grouped[(half, g)], h_codes, h_scales, g, half)
+            for i in range(HALF_TILES * half, HALF_TILES * (half + 1)):
                 b_cols = slice(P * i, P * (i + 1))
                 result = rows.tile([P, D_OUT], F32, tag="rows")
                 for n in range(D_OUT // BANK):
@@ -229,3 +221,21 @@ def tile_autoencoder_pb_kernel(tc, h_dec1, D2, g4, b4, D3, bo, out):
                     nc.vector.tensor_tensor(out=result[:, d_cols], in0=acc[:], in1=bo_all[:, d_cols], op=ALU.add)
                     nc.scalar.activation(out=result[:, d_cols], in_=result[:, d_cols], func=AF.Sigmoid)
                 nc.sync.dma_start(out=out_tiles[i], in_=result[:])
+
+        quantise_units(nc, psum, stage, ident, d2_words, d2_codes, d2_scales, [(0, 0), (0, 1)], both)
+        quantise_units(nc, psum, stage, ident, x_words, x_codes, x_scales, [(0, 0), (0, 1)], both)
+
+        gb_bank = psum.tile([P, BANK], F32, tag="bank")
+        nc.tensor.transpose(gb_bank[:, 0:P], gb_raw[:].bitcast(F32), ident[:])
+        nc.vector.tensor_copy(out=gain_bias[:], in_=gb_bank[:, 0:8].bitcast(BF16))
+
+        for i in range(B_TILES):
+            normalise(*statistics(i))
+        mish_factors(0)
+        mish_factors(1)
+        d3_units = [(g, c) for g in range(PASSES2) for c in range(D_OUT // UNIT)]
+        quantise_units(nc, psum, stage, ident, d3_words, d3_codes, d3_scales, d3_units, vector_only)
+        mish_products(0)
+        second_layer(0)
+        mish_products(1)
+        second_layer(1)

@@ -80,9 +80,9 @@ def tile_autoencoder_pb_kernel(tc, h_dec1, D2, g4, b4, D3, bo, out):
         d2_raw = keep.tile([P, (O1 // P) * K1], BF16)
         d3_raw = keep.tile([P, (D_OUT // P) * O1], BF16)
         load_rows(nc, d2_raw, D2.rearrange("(i p) k -> p i k", p=P))
-        load_rows(nc, x_raw, h_dec1.rearrange("(p i) k -> p i k", p=P))
+        load_rows(nc, x_raw, h_dec1.rearrange("(i p) k -> p i k", p=P))
         load_rows(nc, d3_raw, D3.rearrange("(i p) k -> p i k", p=P))
-        out_tiles = out.rearrange("(p i) d -> i p d", p=P)
+        out_tiles = out.rearrange("(i p) d -> i p d", p=P)
         bo_all = keep.tile([P, D_OUT], BF16)
         nc.sync.dma_start(out=bo_all[:], in_=bo.partition_broadcast(P))
 
@@ -162,7 +162,7 @@ def tile_autoencoder_pb_kernel(tc, h_dec1, D2, g4, b4, D3, bo, out):
                     out=z_blocks, in_=u_blocks, func=AF.Identity, scale=rstd[:, 0:1], bias=shift[:, 0:1]
                 )
 
-        def mish_factors(half):
+        def softplus(half):
             for g in range(PASSES2):
                 for t in range(PACK):
                     c = PACK * g + t
@@ -183,18 +183,19 @@ def tile_autoencoder_pb_kernel(tc, h_dec1, D2, g4, b4, D3, bo, out):
             for g in range(PASSES2):
                 chunk = w[:, half, g].rearrange("p t b -> p (t b)")
                 nc.scalar.activation(out=chunk, in_=chunk, func=AF.Ln, bias=one[:, 0:1])
+
+        def tanh(half):
             for g in range(PASSES2):
                 chunk = w[:, half, g].rearrange("p t b -> p (t b)")
                 nc.scalar.activation(out=chunk, in_=chunk, func=AF.Tanh)
 
         def mish_products(half):
-            engines = (nc.gpsimd, nc.vector)
             for g in range(PASSES2):
                 product = products.tile([P, PACK * BANK], BF16, align_bytes=64)
-                engines[g].tensor_tensor(
-                    out=product[:].rearrange("p (b t) -> p b t", t=PACK),
-                    in0=v[:, half, g].rearrange("p t b -> p b t"),
-                    in1=w[:, half, g].rearrange("p t b -> p b t"),
+                nc.vector.tensor_tensor(
+                    out=product[:].rearrange("p (c i t) -> p c t i", i=4, t=PACK),
+                    in0=v[:, half, g].rearrange("p t (c i) -> p c t i", i=4),
+                    in1=w[:, half, g].rearrange("p t (c i) -> p c t i", i=4),
                     op=ALU.mult,
                 )
                 h_grouped[(half, g)] = product
@@ -224,18 +225,21 @@ def tile_autoencoder_pb_kernel(tc, h_dec1, D2, g4, b4, D3, bo, out):
 
         quantise_units(nc, psum, stage, ident, d2_words, d2_codes, d2_scales, [(0, 0), (0, 1)], both)
         quantise_units(nc, psum, stage, ident, x_words, x_codes, x_scales, [(0, 0), (0, 1)], both)
+        for i in range(B_TILES):
+            normalise(*statistics(i))
 
         gb_bank = psum.tile([P, BANK], F32, tag="bank")
         nc.tensor.transpose(gb_bank[:, 0:P], gb_raw[:].bitcast(F32), ident[:])
         nc.vector.tensor_copy(out=gain_bias[:], in_=gb_bank[:, 0:8].bitcast(BF16))
 
-        for i in range(B_TILES):
-            normalise(*statistics(i))
-        mish_factors(0)
-        mish_factors(1)
+        softplus(0)
+        tanh(0)
+        softplus(1)
+        sigmoid_first = small.tile([P, 1], F32)
+        nc.scalar.activation(out=sigmoid_first[:], in_=one[:], func=AF.Sigmoid)
+        tanh(1)
         d3_units = [(g, c) for g in range(PASSES2) for c in range(D_OUT // UNIT)]
         quantise_units(nc, psum, stage, ident, d3_words, d3_codes, d3_scales, d3_units, vector_only)
-        mish_products(0)
-        second_layer(0)
-        mish_products(1)
-        second_layer(1)
+        for half in range(2):
+            mish_products(half)
+            second_layer(half)

@@ -24,45 +24,7 @@ PASSES2 = O1 // K_PASS
 
 FLOPS = 2 * B * O1 * K1 + 2 * B * D_OUT * O1
 
-
-def load_rows(nc, raw, dram_rows):
-    sbuf_rows = raw[:].rearrange("p (i k) -> p i k", k=dram_rows.shape[2])
-    for c in range(dram_rows.shape[1] // UNIT_TILES):
-        tiles = slice(UNIT_TILES * c, UNIT_TILES * (c + 1))
-        nc.sync.dma_start(out=sbuf_rows[:, tiles, :], in_=dram_rows[:, tiles, :])
-
-
-def regroup_unit(nc, psum, stage, ident, words, g, c, copies):
-    grouped = stage.tile([P, PACK * UNIT], BF16, align_bytes=64)
-    grouped_words = grouped[:].bitcast(F32).rearrange("p (h r u) -> p h r u", h=2, u=2)
-    for h in range(2):
-        bank = psum.tile([P, BANK], F32, tag="bank")
-        planes = bank[:].rearrange("p (u j r) -> p u j r", u=2, j=2)
-        for u in range(2):
-            first_word = (K_PASS // 2) * g + P * u
-            for j in range(2):
-                nc.tensor.transpose(
-                    planes[:, u, j, :],
-                    words[:, UNIT_TILES * c + 2 * h + j, first_word : first_word + P],
-                    ident[:],
-                )
-        copies[h](out=grouped_words[:, h], in_=bank[:].rearrange("p (u r) -> p r u", u=2))
-    return grouped
-
-
-def quantise_unit(nc, grouped, codes, scales, g, c):
-    cols = slice(UNIT * c, UNIT * (c + 1))
-    nc.vector.quantize_mx(out=codes[:, g, cols].bitcast(FP8X4), scales=scales[:, g, cols], in_=grouped[:])
-
-
-def quantise_units(nc, psum, stage, ident, words, codes, scales, units, copies):
-    waiting = None
-    for g, c in units:
-        grouped = regroup_unit(nc, psum, stage, ident, words, g, c, copies)
-        if waiting is not None:
-            quantise_unit(nc, *waiting)
-        waiting = (grouped, codes, scales, g, c)
-    quantise_unit(nc, *waiting)
+N_ON_VECTOR = ()
 
 
 def tile_autoencoder_pb_kernel(tc, h_dec1, D2, g4, b4, D3, bo, out):
@@ -79,9 +41,21 @@ def tile_autoencoder_pb_kernel(tc, h_dec1, D2, g4, b4, D3, bo, out):
         x_raw = keep.tile([P, B_TILES * K1], BF16)
         d2_raw = keep.tile([P, (O1 // P) * K1], BF16)
         d3_raw = keep.tile([P, (D_OUT // P) * O1], BF16)
-        load_rows(nc, d2_raw, D2.rearrange("(i p) k -> p i k", p=P))
-        load_rows(nc, x_raw, h_dec1.rearrange("(i p) k -> p i k", p=P))
-        load_rows(nc, d3_raw, D3.rearrange("(i p) k -> p i k", p=P))
+
+        def load_tiles(raw, dram, first, count):
+            dram_rows = dram.rearrange("(i p) k -> p i k", p=P)
+            sbuf_rows = raw[:].rearrange("p (i k) -> p i k", k=dram_rows.shape[2])
+            tiles = slice(first, first + count)
+            nc.sync.dma_start(out=sbuf_rows[:, tiles, :], in_=dram_rows[:, tiles, :])
+
+        load_tiles(d2_raw, D2, 0, 4)
+        load_tiles(d2_raw, D2, 4, 4)
+        load_tiles(x_raw, h_dec1, 0, 2)
+        load_tiles(x_raw, h_dec1, 2, 2)
+        load_tiles(x_raw, h_dec1, 4, 4)
+        load_tiles(d3_raw, D3, 0, 4)
+        load_tiles(d3_raw, D3, 4, 4)
+        load_tiles(d3_raw, D3, 8, 4)
         out_tiles = out.rearrange("(i p) d -> i p d", p=P)
         bo_all = keep.tile([P, D_OUT], BF16)
         nc.sync.dma_start(out=bo_all[:], in_=bo.partition_broadcast(P))
@@ -112,32 +86,62 @@ def tile_autoencoder_pb_kernel(tc, h_dec1, D2, g4, b4, D3, bo, out):
         h_scales = keep.tile([P, PASSES2, B], U8, align_bytes=64)
 
         gain_bias = keep.tile([P, 16], F32)
-        z = []
+        z = {}
         v = keep.tile([P, 2, PASSES2, PACK, BANK], F32)
         w = keep.tile([P, 2, PASSES2, PACK, BANK], F32)
         h_grouped = {}
 
-        both = (nc.scalar.copy, nc.vector.tensor_copy)
-        vector_only = (nc.vector.tensor_copy, nc.vector.tensor_copy)
+        S, V = nc.scalar.copy, nc.vector.tensor_copy
 
-        def statistics(i):
+        def open_unit(g, first, banks):
+            grouped = stage.tile([P, PACK * 2 * P * banks], BF16, align_bytes=64, tag="grouped")
+            return grouped, g, first, 2 * banks
+
+        def fill(unit, words, h, copy):
+            grouped, g, first, count = unit
+            grouped_words = grouped[:].bitcast(F32).rearrange("p (h r u) -> p h r u", h=count // 2, u=2)
+            bank = psum.tile([P, BANK], F32, tag="bank")
+            planes = bank[:].rearrange("p (u j r) -> p u j r", u=2, j=2)
+            for u in range(2):
+                first_word = (K_PASS // 2) * g + P * u
+                for j in range(2):
+                    nc.tensor.transpose(
+                        planes[:, u, j, :],
+                        words[:, first + 2 * h + j, first_word : first_word + P],
+                        ident[:],
+                    )
+            copy(out=grouped_words[:, h], in_=bank[:].rearrange("p (u r) -> p r u", u=2))
+
+        def regroup(words, g, first, copies):
+            unit = open_unit(g, first, len(copies))
+            for h in range(len(copies)):
+                fill(unit, words, h, copies[h])
+            return unit
+
+        def quantise(unit, codes, scales):
+            grouped, g, first, count = unit
+            cols = slice(P * first, P * (first + count))
+            nc.vector.quantize_mx(out=codes[:, g, cols].bitcast(FP8X4), scales=scales[:, g, cols], in_=grouped[:])
+
+        def first_matmul(i, n):
             b_cols = slice(P * i, P * (i + 1))
+            o_cols = slice(BANK * n, BANK * (n + 1))
+            u = psum.tile([P, BANK], F32, tag="bank")
+            nc.tensor.matmul_mx(
+                out=u[:],
+                lhsT=x_codes[:, 0, b_cols].bitcast(FP8X4),
+                lhsT_scale=x_scales[:, 0, b_cols],
+                rhs=d2_codes[:, 0, o_cols].bitcast(FP8X4),
+                rhs_scale=d2_scales[:, 0, o_cols],
+                start=True,
+                stop=True,
+            )
+            return u
+
+        def statistics(u_banks):
             stats = small.tile([P, 2, 6], F32)
-            u_banks = []
-            for n in range(O1 // BANK):
-                o_cols = slice(BANK * n, BANK * (n + 1))
-                u = psum.tile([P, BANK], F32, tag="bank")
-                nc.tensor.matmul_mx(
-                    out=u[:],
-                    lhsT=x_codes[:, 0, b_cols].bitcast(FP8X4),
-                    lhsT_scale=x_scales[:, 0, b_cols],
-                    rhs=d2_codes[:, 0, o_cols].bitcast(FP8X4),
-                    rhs_scale=d2_scales[:, 0, o_cols],
-                    start=True,
-                    stop=True,
-                )
-                nc.vector.bn_stats(out=stats[:, n, :], in_=u[:])
-                u_banks.append(u)
+            for n in range(2):
+                nc.vector.bn_stats(out=stats[:, n, :], in_=u_banks[n][:])
             mean_var = small.tile([P, 2], F32)
             nc.vector.bn_aggr(out=mean_var[:], in_=stats[:].rearrange("p n s -> p (n s)"))
             var_eps = small.tile([P, 1], F32)
@@ -150,19 +154,28 @@ def tile_autoencoder_pb_kernel(tc, h_dec1, D2, g4, b4, D3, bo, out):
             nc.gpsimd.tensor_scalar(
                 out=shift[:], in0=mean_var[:, 0:1], scalar1=rstd[:, 0:1], scalar2=-1.0, op0=ALU.mult, op1=ALU.mult
             )
-            return u_banks, rstd, shift
+            return rstd, shift
 
-        def normalise(u_banks, rstd, shift):
+        def normalise(i, u_banks, rstd, shift):
             z_tile = rows.tile([P, O1], F32, tag="rows")
-            z.append(z_tile)
+            z[i] = z_tile
             for n in range(O1 // BANK):
                 z_blocks = z_tile[:, BANK * n : BANK * (n + 1)].rearrange("p (m e q) -> p m e q", m=2, e=2)
                 u_blocks = u_banks[n][:].rearrange("p (m q e) -> p m e q", m=2, e=2)
-                nc.scalar.activation(
-                    out=z_blocks, in_=u_blocks, func=AF.Identity, scale=rstd[:, 0:1], bias=shift[:, 0:1]
-                )
+                if i in N_ON_VECTOR:
+                    nc.vector.tensor_scalar(
+                        out=z_blocks, in0=u_blocks, scalar1=rstd[:, 0:1], scalar2=shift[:, 0:1], op0=ALU.mult, op1=ALU.add
+                    )
+                else:
+                    nc.scalar.activation(
+                        out=z_blocks, in_=u_blocks, func=AF.Identity, scale=rstd[:, 0:1], bias=shift[:, 0:1]
+                    )
 
-        def softplus(half):
+        def first_layer(i):
+            u_banks = [first_matmul(i, n) for n in range(2)]
+            normalise(i, u_banks, *statistics(u_banks))
+
+        def exponentials(half):
             for g in range(PASSES2):
                 for t in range(PACK):
                     c = PACK * g + t
@@ -180,6 +193,8 @@ def tile_autoencoder_pb_kernel(tc, h_dec1, D2, g4, b4, D3, bo, out):
                         op1=ALU.add,
                     )
                     nc.scalar.activation(out=w[:, half, g, t, :], in_=v[:, half, g, t, :], func=AF.Exp)
+
+        def logarithms(half):
             for g in range(PASSES2):
                 chunk = w[:, half, g].rearrange("p t b -> p (t b)")
                 nc.scalar.activation(out=chunk, in_=chunk, func=AF.Ln, bias=one[:, 0:1])
@@ -189,57 +204,95 @@ def tile_autoencoder_pb_kernel(tc, h_dec1, D2, g4, b4, D3, bo, out):
                 chunk = w[:, half, g].rearrange("p t b -> p (t b)")
                 nc.scalar.activation(out=chunk, in_=chunk, func=AF.Tanh)
 
-        def mish_products(half):
-            for g in range(PASSES2):
-                product = products.tile([P, PACK * BANK], BF16, align_bytes=64)
-                nc.vector.tensor_tensor(
-                    out=product[:].rearrange("p (c i t) -> p c t i", i=4, t=PACK),
-                    in0=v[:, half, g].rearrange("p t (c i) -> p c t i", i=4),
-                    in1=w[:, half, g].rearrange("p t (c i) -> p c t i", i=4),
-                    op=ALU.mult,
-                )
-                h_grouped[(half, g)] = product
+        def mish_product(first, tiles, g, engine):
+            half, j = divmod(first, HALF_TILES)
+            b_cols = slice(P * j, P * (j + tiles))
+            product = products.tile([P, PACK * P * tiles], BF16, align_bytes=64, tag="product")
+            engine.tensor_tensor(
+                out=product[:].rearrange("p (c i t) -> p c t i", i=4, t=PACK),
+                in0=v[:, half, g, :, b_cols].rearrange("p t (c i) -> p c t i", i=4),
+                in1=w[:, half, g, :, b_cols].rearrange("p t (c i) -> p c t i", i=4),
+                op=ALU.mult,
+            )
+            h_grouped[(first, g)] = (product, tiles)
 
-        def second_layer(half):
-            for g in range(PASSES2):
-                quantise_unit(nc, h_grouped[(half, g)], h_codes, h_scales, g, half)
-            for i in range(HALF_TILES * half, HALF_TILES * (half + 1)):
-                b_cols = slice(P * i, P * (i + 1))
-                result = rows.tile([P, D_OUT], F32, tag="rows")
-                for n in range(D_OUT // BANK):
-                    d_cols = slice(BANK * n, BANK * (n + 1))
-                    acc = psum.tile([P, BANK], F32, tag="bank")
-                    for g in range(PASSES2):
-                        nc.tensor.matmul_mx(
-                            out=acc[:],
-                            lhsT=h_codes[:, g, b_cols].bitcast(FP8X4),
-                            lhsT_scale=h_scales[:, g, b_cols],
-                            rhs=d3_codes[:, g, d_cols].bitcast(FP8X4),
-                            rhs_scale=d3_scales[:, g, d_cols],
-                            start=(g == 0),
-                            stop=(g == PASSES2 - 1),
-                        )
-                    nc.vector.tensor_tensor(out=result[:, d_cols], in0=acc[:], in1=bo_all[:, d_cols], op=ALU.add)
-                    nc.scalar.activation(out=result[:, d_cols], in_=result[:, d_cols], func=AF.Sigmoid)
+        def quantise_h(first, g):
+            product, tiles = h_grouped[(first, g)]
+            b_cols = slice(P * first, P * (first + tiles))
+            nc.vector.quantize_mx(
+                out=h_codes[:, g, b_cols].bitcast(FP8X4), scales=h_scales[:, g, b_cols], in_=product[:]
+            )
+
+        def second_layer(i, split_store=False):
+            b_cols = slice(P * i, P * (i + 1))
+            result = rows.tile([P, D_OUT], F32, tag="rows")
+            for n in range(D_OUT // BANK):
+                d_cols = slice(BANK * n, BANK * (n + 1))
+                acc = psum.tile([P, BANK], F32, tag="bank")
+                for g in range(PASSES2):
+                    nc.tensor.matmul_mx(
+                        out=acc[:],
+                        lhsT=h_codes[:, g, b_cols].bitcast(FP8X4),
+                        lhsT_scale=h_scales[:, g, b_cols],
+                        rhs=d3_codes[:, g, d_cols].bitcast(FP8X4),
+                        rhs_scale=d3_scales[:, g, d_cols],
+                        start=(g == 0),
+                        stop=(g == PASSES2 - 1),
+                    )
+                nc.vector.tensor_tensor(out=result[:, d_cols], in0=acc[:], in1=bo_all[:, d_cols], op=ALU.add)
+                nc.scalar.activation(out=result[:, d_cols], in_=result[:, d_cols], func=AF.Sigmoid)
+                if split_store:
+                    nc.sync.dma_start(out=out_tiles[i][:, d_cols], in_=result[:, d_cols])
+            if not split_store:
                 nc.sync.dma_start(out=out_tiles[i], in_=result[:])
 
-        quantise_units(nc, psum, stage, ident, d2_words, d2_codes, d2_scales, [(0, 0), (0, 1)], both)
-        quantise_units(nc, psum, stage, ident, x_words, x_codes, x_scales, [(0, 0), (0, 1)], both)
-        for i in range(B_TILES):
-            normalise(*statistics(i))
+        d20 = regroup(d2_words, 0, 0, (S, S))
+        d21 = regroup(d2_words, 0, 4, (S, S))
+        quantise(d20, d2_codes, d2_scales)
+        x0 = regroup(x_words, 0, 0, (S,))
+        quantise(d21, d2_codes, d2_scales)
+        x1 = regroup(x_words, 0, 2, (S,))
+        quantise(x0, x_codes, x_scales)
+        u0 = [first_matmul(0, n) for n in range(2)]
+        u1 = [first_matmul(1, n) for n in range(2)]
+        x2 = regroup(x_words, 0, 4, (S, S))
+        st0 = statistics(u0)
+        quantise(x1, x_codes, x_scales)
+        st1 = statistics(u1)
+        normalise(0, u0, *st0)
+        u2 = [first_matmul(2, n) for n in range(2)]
+        st2 = statistics(u2)
+        quantise(x2, x_codes, x_scales)
+        normalise(1, u1, *st1)
+        normalise(2, u2, *st2)
+        for i in range(3, B_TILES):
+            first_layer(i)
 
         gb_bank = psum.tile([P, BANK], F32, tag="bank")
         nc.tensor.transpose(gb_bank[:, 0:P], gb_raw[:].bitcast(F32), ident[:])
         nc.vector.tensor_copy(out=gain_bias[:], in_=gb_bank[:, 0:8].bitcast(BF16))
 
-        softplus(0)
+        exponentials(0)
+        logarithms(0)
         tanh(0)
-        softplus(1)
+        exponentials(1)
+        logarithms(1)
         sigmoid_first = small.tile([P, 1], F32)
         nc.scalar.activation(out=sigmoid_first[:], in_=one[:], func=AF.Sigmoid)
         tanh(1)
-        d3_units = [(g, c) for g in range(PASSES2) for c in range(D_OUT // UNIT)]
-        quantise_units(nc, psum, stage, ident, d3_words, d3_codes, d3_scales, d3_units, vector_only)
+        waiting = None
+        for first in (0, 4, 8):
+            for g in range(PASSES2):
+                unit = regroup(d3_words, g, first, (V, V))
+                if waiting is not None:
+                    quantise(waiting, d3_codes, d3_scales)
+                waiting = unit
+        quantise(waiting, d3_codes, d3_scales)
         for half in range(2):
-            mish_products(half)
-            second_layer(half)
+            first = HALF_TILES * half
+            for g in range(PASSES2):
+                mish_product(first, HALF_TILES, g, nc.vector)
+            for g in range(PASSES2):
+                quantise_h(first, g)
+            for i in range(first, first + HALF_TILES):
+                second_layer(i, split_store=False)

@@ -42,21 +42,23 @@ def tile_autoencoder_pb_kernel(tc, h_dec1, D2, g4, b4, D3, bo, out):
         d2_raw = keep.tile([P, (O1 // P) * K1], BF16)
         d3_raw = keep.tile([P, (D_OUT // P) * O1], BF16)
 
-        def load_tiles(raw, dram, first, count):
-            dram_rows = dram.rearrange("(i p) k -> p i k", p=P)
+        def load_tiles(raw, dram_rows, first, count):
             sbuf_rows = raw[:].rearrange("p (i k) -> p i k", k=dram_rows.shape[2])
             tiles = slice(first, first + count)
             nc.sync.dma_start(out=sbuf_rows[:, tiles, :], in_=dram_rows[:, tiles, :])
 
-        load_tiles(d2_raw, D2, 0, 4)
-        load_tiles(d2_raw, D2, 4, 4)
-        load_tiles(x_raw, h_dec1, 0, 2)
-        load_tiles(x_raw, h_dec1, 2, 2)
-        load_tiles(x_raw, h_dec1, 4, 4)
-        load_tiles(d3_raw, D3, 0, 4)
-        load_tiles(d3_raw, D3, 4, 4)
-        load_tiles(d3_raw, D3, 8, 4)
-        out_tiles = out.rearrange("(i p) d -> i p d", p=P)
+        d2_rows = D2.rearrange("(m p e) k -> p m (e k)", p=P, e=2)
+        x_rows = h_dec1.rearrange("(p i) k -> p i k", p=P)
+        d3_rows = D3.rearrange("(i p) k -> p i k", p=P)
+        load_tiles(d2_raw, d2_rows, 0, 2)
+        load_tiles(d2_raw, d2_rows, 2, 2)
+        load_tiles(x_raw, x_rows, 0, 2)
+        load_tiles(x_raw, x_rows, 2, 2)
+        load_tiles(x_raw, x_rows, 4, 4)
+        load_tiles(d3_raw, d3_rows, 0, 4)
+        load_tiles(d3_raw, d3_rows, 4, 4)
+        load_tiles(d3_raw, d3_rows, 8, 4)
+        out_tiles = out.rearrange("(p i) d -> i p d", p=P)
         bo_all = keep.tile([P, D_OUT], BF16)
         nc.sync.dma_start(out=bo_all[:], in_=bo.partition_broadcast(P))
 
@@ -160,8 +162,8 @@ def tile_autoencoder_pb_kernel(tc, h_dec1, D2, g4, b4, D3, bo, out):
             z_tile = rows.tile([P, O1], F32, tag="rows")
             z[i] = z_tile
             for n in range(O1 // BANK):
-                z_blocks = z_tile[:, BANK * n : BANK * (n + 1)].rearrange("p (m e q) -> p m e q", m=2, e=2)
-                u_blocks = u_banks[n][:].rearrange("p (m q e) -> p m e q", m=2, e=2)
+                z_blocks = z_tile[:, BANK * n : BANK * (n + 1)]
+                u_blocks = u_banks[n][:]
                 if i in N_ON_VECTOR:
                     nc.vector.tensor_scalar(
                         out=z_blocks, in0=u_blocks, scalar1=rstd[:, 0:1], scalar2=shift[:, 0:1], op0=ALU.mult, op1=ALU.add
@@ -192,7 +194,13 @@ def tile_autoencoder_pb_kernel(tc, h_dec1, D2, g4, b4, D3, bo, out):
                         op0=ALU.mult,
                         op1=ALU.add,
                     )
-                    nc.scalar.activation(out=w[:, half, g, t, :], in_=v[:, half, g, t, :], func=AF.Exp)
+                    if t % 2 == 1:
+                        pair = slice(t - 1, t + 1)
+                        nc.scalar.activation(
+                            out=w[:, half, g, pair, :].rearrange("p t b -> p (t b)"),
+                            in_=v[:, half, g, pair, :].rearrange("p t b -> p (t b)"),
+                            func=AF.Exp,
+                        )
 
         def logarithms(half):
             for g in range(PASSES2):

@@ -50,8 +50,8 @@ def tile_autoencoder_pb_kernel(tc, h_dec1, D2, g4, b4, D3, bo, out):
         d2_rows = D2.rearrange("(m p e) k -> p m (e k)", p=P, e=2)
         x_rows = h_dec1.rearrange("(p i) k -> p i k", p=P)
         d3_rows = D3.rearrange("(i p) k -> p i k", p=P)
-        load_tiles(d2_raw, d2_rows, 0, 2)
-        load_tiles(d2_raw, d2_rows, 2, 2)
+        for m in range(4):
+            load_tiles(d2_raw, d2_rows, m, 1)
         load_tiles(x_raw, x_rows, 0, 2)
         load_tiles(x_raw, x_rows, 2, 2)
         load_tiles(x_raw, x_rows, 4, 4)

@@ -25,13 +25,14 @@ PASSES2 = O1 // K_PASS
 FLOPS = 2 * B * O1 * K1 + 2 * B * D_OUT * O1
 
 N_ON_VECTOR = ()
+HEAD = (("d", 0), ("d", 1), ("d", 2), ("x", 0), ("d", 3))
 
 
 def tile_autoencoder_pb_kernel(tc, h_dec1, D2, g4, b4, D3, bo, out):
     nc = tc.nc
     with (
         tc.tile_pool(name="keep", bufs=1) as keep,
-        tc.tile_pool(name="stage", bufs=4) as stage,
+        tc.tile_pool(name="stage", bufs=6) as stage,
         tc.tile_pool(name="products", bufs=4) as products,
         tc.tile_pool(name="small", bufs=4) as small,
         tc.tile_pool(name="rows", bufs=B_TILES) as rows,
@@ -50,9 +51,11 @@ def tile_autoencoder_pb_kernel(tc, h_dec1, D2, g4, b4, D3, bo, out):
         d2_rows = D2.rearrange("(m p e) k -> p m (e k)", p=P, e=2)
         x_rows = h_dec1.rearrange("(p i) k -> p i k", p=P)
         d3_rows = D3.rearrange("(i p) k -> p i k", p=P)
-        for m in range(4):
-            load_tiles(d2_raw, d2_rows, m, 1)
-        load_tiles(x_raw, x_rows, 0, 2)
+        for kind, m in HEAD:
+            if kind == "d":
+                load_tiles(d2_raw, d2_rows, m, 1)
+            else:
+                load_tiles(x_raw, x_rows, 0, 2)
         load_tiles(x_raw, x_rows, 2, 2)
         load_tiles(x_raw, x_rows, 4, 4)
         load_tiles(d3_raw, d3_rows, 0, 4)
@@ -254,13 +257,17 @@ def tile_autoencoder_pb_kernel(tc, h_dec1, D2, g4, b4, D3, bo, out):
             if not split_store:
                 nc.sync.dma_start(out=out_tiles[i], in_=result[:])
 
-        d20 = regroup(d2_words, 0, 0, (S, S))
-        d21 = regroup(d2_words, 0, 4, (S, S))
-        quantise(d20, d2_codes, d2_scales)
-        x0 = regroup(x_words, 0, 0, (S,))
-        quantise(d21, d2_codes, d2_scales)
+        waiting_head = None
+        for kind, m in HEAD:
+            if kind == "d":
+                unit = (regroup(d2_words, 0, 2 * m, (S,)), d2_codes, d2_scales)
+            else:
+                unit = (regroup(x_words, 0, 0, (S,)), x_codes, x_scales)
+            if waiting_head is not None:
+                quantise(*waiting_head)
+            waiting_head = unit
         x1 = regroup(x_words, 0, 2, (S,))
-        quantise(x0, x_codes, x_scales)
+        quantise(*waiting_head)
         u0 = [first_matmul(0, n) for n in range(2)]
         u1 = [first_matmul(1, n) for n in range(2)]
         x2 = regroup(x_words, 0, 4, (S, S))

import concourse.mybir as mybir
from concourse.masks import make_identity

F32 = mybir.dt.float32
BF16 = mybir.dt.bfloat16
U32 = mybir.dt.uint32
U8 = mybir.dt.uint8
FP8X4 = mybir.dt.float8_e4m3fn_x4
AF = mybir.ActivationFunctionType
ALU = mybir.AluOpType

P = 128
PACK = 4
K_PASS = P * PACK
BANK = 512
UNIT = 512
UNIT_TILES = UNIT // P

B, K1, O1, D_OUT = 1024, 512, 1024, 1536
EPS = 1e-5
B_TILES = B // P
HALF_TILES = BANK // P
PASSES2 = O1 // K_PASS

FLOPS = 2 * B * O1 * K1 + 2 * B * D_OUT * O1

N_ON_VECTOR = ()
HEAD = (("d", 0), ("d", 1), ("d", 2), ("x", 0), ("d", 3))


def tile_autoencoder_pb_kernel(tc, h_dec1, D2, g4, b4, D3, bo, out):
    nc = tc.nc
    with (
        tc.tile_pool(name="keep", bufs=1) as keep,
        tc.tile_pool(name="stage", bufs=6) as stage,
        tc.tile_pool(name="products", bufs=4) as products,
        tc.tile_pool(name="small", bufs=4) as small,
        tc.tile_pool(name="rows", bufs=B_TILES) as rows,
        tc.psum_pool(name="psum", bufs=8) as psum,
        tc.manual_schedule(),
    ):
        x_raw = keep.tile([P, B_TILES * K1], BF16)
        d2_raw = keep.tile([P, (O1 // P) * K1], BF16)
        d3_raw = keep.tile([P, (D_OUT // P) * O1], BF16)

        def load_tiles(raw, dram_rows, first, count):
            sbuf_rows = raw[:].rearrange("p (i k) -> p i k", k=dram_rows.shape[2])
            tiles = slice(first, first + count)
            nc.sync.dma_start(out=sbuf_rows[:, tiles, :], in_=dram_rows[:, tiles, :])

        d2_rows = D2.rearrange("(m p e) k -> p m (e k)", p=P, e=2)
        x_rows = h_dec1.rearrange("(p i) k -> p i k", p=P)
        d3_rows = D3.rearrange("(i p) k -> p i k", p=P)
        for kind, m in HEAD:
            if kind == "d":
                load_tiles(d2_raw, d2_rows, m, 1)
            else:
                load_tiles(x_raw, x_rows, 0, 2)
        load_tiles(x_raw, x_rows, 2, 2)
        load_tiles(x_raw, x_rows, 4, 4)
        load_tiles(d3_raw, d3_rows, 0, 4)
        load_tiles(d3_raw, d3_rows, 4, 4)
        load_tiles(d3_raw, d3_rows, 8, 4)
        out_tiles = out.rearrange("(p i) d -> i p d", p=P)
        bo_all = keep.tile([P, D_OUT], BF16)
        nc.sync.dma_start(out=bo_all[:], in_=bo.partition_broadcast(P))

        gb_raw = keep.tile([P, 2 * P], BF16)
        nc.vector.memset(gb_raw[:], 0.0)
        nc.scalar.dma_start(out=gb_raw[0:4, :], in_=g4.rearrange("(m w) -> m w", m=4))
        nc.scalar.dma_start(out=gb_raw[4:8, :], in_=b4.rearrange("(m w) -> m w", m=4))

        ident = keep.tile([P, P], F32)
        make_identity(nc, ident[:])
        minus_half = keep.tile([P, 1], F32)
        nc.gpsimd.memset(minus_half[:], -0.5)
        one = keep.tile([P, 1], F32)
        nc.gpsimd.memset(one[:], 1.0)

        x_words = x_raw[:].bitcast(F32).rearrange("p (i w) -> p i w", w=K1 // 2)
        d2_words = d2_raw[:].bitcast(F32).rearrange("p (i w) -> p i w", w=K1 // 2)
        d3_words = d3_raw[:].bitcast(F32).rearrange("p (i w) -> p i w", w=O1 // 2)

        x_codes = keep.tile([P, 1, B], U32, align_bytes=64)
        x_scales = keep.tile([P, 1, B], U8, align_bytes=64)
        d2_codes = keep.tile([P, 1, O1], U32, align_bytes=64)
        d2_scales = keep.tile([P, 1, O1], U8, align_bytes=64)
        d3_codes = keep.tile([P, PASSES2, D_OUT], U32, align_bytes=64)
        d3_scales = keep.tile([P, PASSES2, D_OUT], U8, align_bytes=64)
        h_codes = keep.tile([P, PASSES2, B], U32, align_bytes=64)
        h_scales = keep.tile([P, PASSES2, B], U8, align_bytes=64)

        gain_bias = keep.tile([P, 16], F32)
        z = {}
        v = keep.tile([P, 2, PASSES2, PACK, BANK], F32)
        w = keep.tile([P, 2, PASSES2, PACK, BANK], F32)
        h_grouped = {}

        S, V = nc.scalar.copy, nc.vector.tensor_copy

        def open_unit(g, first, banks):
            grouped = stage.tile([P, PACK * 2 * P * banks], BF16, align_bytes=64, tag="grouped")
            return grouped, g, first, 2 * banks

        def fill(unit, words, h, copy):
            grouped, g, first, count = unit
            grouped_words = grouped[:].bitcast(F32).rearrange("p (h r u) -> p h r u", h=count // 2, u=2)
            bank = psum.tile([P, BANK], F32, tag="bank")
            planes = bank[:].rearrange("p (u j r) -> p u j r", u=2, j=2)
            for u in range(2):
                first_word = (K_PASS // 2) * g + P * u
                for j in range(2):
                    nc.tensor.transpose(
                        planes[:, u, j, :],
                        words[:, first + 2 * h + j, first_word : first_word + P],
                        ident[:],
                    )
            copy(out=grouped_words[:, h], in_=bank[:].rearrange("p (u r) -> p r u", u=2))

        def regroup(words, g, first, copies):
            unit = open_unit(g, first, len(copies))
            for h in range(len(copies)):
                fill(unit, words, h, copies[h])
            return unit

        def quantise(unit, codes, scales):
            grouped, g, first, count = unit
            cols = slice(P * first, P * (first + count))
            nc.vector.quantize_mx(out=codes[:, g, cols].bitcast(FP8X4), scales=scales[:, g, cols], in_=grouped[:])

        def first_matmul(i, n):
            b_cols = slice(P * i, P * (i + 1))
            o_cols = slice(BANK * n, BANK * (n + 1))
            u = psum.tile([P, BANK], F32, tag="bank")
            nc.tensor.matmul_mx(
                out=u[:],
                lhsT=x_codes[:, 0, b_cols].bitcast(FP8X4),
                lhsT_scale=x_scales[:, 0, b_cols],
                rhs=d2_codes[:, 0, o_cols].bitcast(FP8X4),
                rhs_scale=d2_scales[:, 0, o_cols],
                start=True,
                stop=True,
            )
            return u

        def statistics(u_banks):
            stats = small.tile([P, 2, 6], F32)
            for n in range(2):
                nc.vector.bn_stats(out=stats[:, n, :], in_=u_banks[n][:])
            mean_var = small.tile([P, 2], F32)
            nc.vector.bn_aggr(out=mean_var[:], in_=stats[:].rearrange("p n s -> p (n s)"))
            var_eps = small.tile([P, 1], F32)
            nc.gpsimd.tensor_scalar(
                out=var_eps[:], in0=mean_var[:, 1:2], scalar1=1.0, scalar2=EPS, op0=ALU.mult, op1=ALU.add
            )
            rstd = small.tile([P, 1], F32)
            nc.gpsimd.tensor_tensor(out=rstd[:], in0=var_eps[:], in1=minus_half[:], op=ALU.pow)
            shift = small.tile([P, 1], F32)
            nc.gpsimd.tensor_scalar(
                out=shift[:], in0=mean_var[:, 0:1], scalar1=rstd[:, 0:1], scalar2=-1.0, op0=ALU.mult, op1=ALU.mult
            )
            return rstd, shift

        def normalise(i, u_banks, rstd, shift):
            z_tile = rows.tile([P, O1], F32, tag="rows")
            z[i] = z_tile
            for n in range(O1 // BANK):
                z_blocks = z_tile[:, BANK * n : BANK * (n + 1)]
                u_blocks = u_banks[n][:]
                if i in N_ON_VECTOR:
                    nc.vector.tensor_scalar(
                        out=z_blocks, in0=u_blocks, scalar1=rstd[:, 0:1], scalar2=shift[:, 0:1], op0=ALU.mult, op1=ALU.add
                    )
                else:
                    nc.scalar.activation(
                        out=z_blocks, in_=u_blocks, func=AF.Identity, scale=rstd[:, 0:1], bias=shift[:, 0:1]
                    )

        def first_layer(i):
            u_banks = [first_matmul(i, n) for n in range(2)]
            normalise(i, u_banks, *statistics(u_banks))

        def exponentials(half):
            for g in range(PASSES2):
                for t in range(PACK):
                    c = PACK * g + t
                    zT = psum.tile([P, BANK], F32, tag="bank")
                    for j in range(HALF_TILES):
                        nc.tensor.transpose(
                            zT[:, P * j : P * (j + 1)], z[HALF_TILES * half + j][:, P * c : P * (c + 1)], ident[:]
                        )
                    nc.vector.tensor_scalar(
                        out=v[:, half, g, t, :],
                        in0=zT[:],
                        scalar1=gain_bias[:, c : c + 1],
                        scalar2=gain_bias[:, 8 + c : 9 + c],
                        op0=ALU.mult,
                        op1=ALU.add,
                    )
                    if t % 2 == 1:
                        pair = slice(t - 1, t + 1)
                        nc.scalar.activation(
                            out=w[:, half, g, pair, :].rearrange("p t b -> p (t b)"),
                            in_=v[:, half, g, pair, :].rearrange("p t b -> p (t b)"),
                            func=AF.Exp,
                        )

        def logarithms(half):
            for g in range(PASSES2):
                chunk = w[:, half, g].rearrange("p t b -> p (t b)")
                nc.scalar.activation(out=chunk, in_=chunk, func=AF.Ln, bias=one[:, 0:1])

        def tanh(half):
            for g in range(PASSES2):
                chunk = w[:, half, g].rearrange("p t b -> p (t b)")
                nc.scalar.activation(out=chunk, in_=chunk, func=AF.Tanh)

        def mish_product(first, tiles, g, engine):
            half, j = divmod(first, HALF_TILES)
            b_cols = slice(P * j, P * (j + tiles))
            product = products.tile([P, PACK * P * tiles], BF16, align_bytes=64, tag="product")
            engine.tensor_tensor(
                out=product[:].rearrange("p (c i t) -> p c t i", i=4, t=PACK),
                in0=v[:, half, g, :, b_cols].rearrange("p t (c i) -> p c t i", i=4),
                in1=w[:, half, g, :, b_cols].rearrange("p t (c i) -> p c t i", i=4),
                op=ALU.mult,
            )
            h_grouped[(first, g)] = (product, tiles)

        def quantise_h(first, g):
            product, tiles = h_grouped[(first, g)]
            b_cols = slice(P * first, P * (first + tiles))
            nc.vector.quantize_mx(
                out=h_codes[:, g, b_cols].bitcast(FP8X4), scales=h_scales[:, g, b_cols], in_=product[:]
            )

        def second_layer(i, split_store=False):
            b_cols = slice(P * i, P * (i + 1))
            result = rows.tile([P, D_OUT], F32, tag="rows")
            for n in range(D_OUT // BANK):
                d_cols = slice(BANK * n, BANK * (n + 1))
                acc = psum.tile([P, BANK], F32, tag="bank")
                for g in range(PASSES2):
                    nc.tensor.matmul_mx(
                        out=acc[:],
                        lhsT=h_codes[:, g, b_cols].bitcast(FP8X4),
                        lhsT_scale=h_scales[:, g, b_cols],
                        rhs=d3_codes[:, g, d_cols].bitcast(FP8X4),
                        rhs_scale=d3_scales[:, g, d_cols],
                        start=(g == 0),
                        stop=(g == PASSES2 - 1),
                    )
                nc.vector.tensor_tensor(out=result[:, d_cols], in0=acc[:], in1=bo_all[:, d_cols], op=ALU.add)
                nc.scalar.activation(out=result[:, d_cols], in_=result[:, d_cols], func=AF.Sigmoid)
                if split_store:
                    nc.sync.dma_start(out=out_tiles[i][:, d_cols], in_=result[:, d_cols])
            if not split_store:
                nc.sync.dma_start(out=out_tiles[i], in_=result[:])

        waiting_head = None
        for kind, m in HEAD:
            if kind == "d":
                unit = (regroup(d2_words, 0, 2 * m, (S,)), d2_codes, d2_scales)
            else:
                unit = (regroup(x_words, 0, 0, (S,)), x_codes, x_scales)
            if waiting_head is not None:
                quantise(*waiting_head)
            waiting_head = unit
        x1 = regroup(x_words, 0, 2, (S,))
        quantise(*waiting_head)
        u0 = [first_matmul(0, n) for n in range(2)]
        u1 = [first_matmul(1, n) for n in range(2)]
        x2 = regroup(x_words, 0, 4, (S, S))
        st0 = statistics(u0)
        quantise(x1, x_codes, x_scales)
        st1 = statistics(u1)
        normalise(0, u0, *st0)
        u2 = [first_matmul(2, n) for n in range(2)]
        st2 = statistics(u2)
        quantise(x2, x_codes, x_scales)
        normalise(1, u1, *st1)
        normalise(2, u2, *st2)
        for i in range(3, B_TILES):
            first_layer(i)

        gb_bank = psum.tile([P, BANK], F32, tag="bank")
        nc.tensor.transpose(gb_bank[:, 0:P], gb_raw[:].bitcast(F32), ident[:])
        nc.vector.tensor_copy(out=gain_bias[:], in_=gb_bank[:, 0:8].bitcast(BF16))

        exponentials(0)
        logarithms(0)
        tanh(0)
        exponentials(1)
        logarithms(1)
        sigmoid_first = small.tile([P, 1], F32)
        nc.scalar.activation(out=sigmoid_first[:], in_=one[:], func=AF.Sigmoid)
        tanh(1)
        waiting = None
        for first in (0, 4, 8):
            for g in range(PASSES2):
                unit = regroup(d3_words, g, first, (V, V))
                if waiting is not None:
                    quantise(waiting, d3_codes, d3_scales)
                waiting = unit
        quantise(waiting, d3_codes, d3_scales)
        for half in range(2):
            first = HALF_TILES * half
            for g in range(PASSES2):
                mish_product(first, HALF_TILES, g, nc.vector)
            for g in range(PASSES2):
                quantise_h(first, g)
            for i in range(first, first + HALF_TILES):
                second_layer(i, split_store=False)
